import numpy as np
import ml_dtypes


def mxq(x, axis, fmt="e4m3"):
    dtype, down = {"e4m3": (ml_dtypes.float8_e4m3fn, 7), "e5m2": (ml_dtypes.float8_e5m2, 14)}[fmt]
    v = np.moveaxis(np.asarray(x, np.float32).astype(ml_dtypes.bfloat16).astype(np.float64), axis, -1)
    blocks = v.reshape(v.shape[:-1] + (-1, 32))
    amax = np.abs(blocks).max(-1, keepdims=True)
    byte = np.maximum(np.where(amax > 0, np.frexp(amax)[1] - 1 + 127, 0) - down, 1)
    scale = np.exp2(byte - 127.0)
    codes = (blocks / scale).astype(np.float32).astype(dtype).astype(np.float64)
    return np.moveaxis((codes * scale).reshape(v.shape), -1, axis)


WIDE = False


def mx_kscale(k):
    if not WIDE:
        return np.ones(k)
    levels = np.array([10, -10, 5, -5, 0])
    a = np.random.permutation(np.resize(levels, k // 512 * 4)).reshape(k // 512, 4)
    idx = np.arange(k)
    return np.exp2(a[idx // 512, idx % 128 // 32])


BF16 = ml_dtypes.bfloat16


def bf(x):
    return np.asarray(x, np.float32).astype(BF16)


def f64(x):
    return np.asarray(x).astype(np.float64)


E2M1 = np.array([0.0, 0.5, 1.0, 1.5, 2.0, 3.0, 4.0, 6.0, -0.0, -0.5, -1.0, -1.5, -2.0, -3.0, -4.0, -6.0])


def pack_weight(w, fmt):
    k, n = w.shape
    w = f64(bf(w)).reshape(k // 32, 32, n)
    amax = np.abs(w).max(1)
    if fmt == "e4m3":
        byte = np.frexp(amax)[1] - 1 + 127 - 7
    else:
        mant, ex = np.frexp(amax / 6.0)
        byte = np.where(mant > 0.5, ex, ex - 1) + 127
    byte = np.clip(np.where(amax > 0, byte, 1), 1, 254)
    scaled = (w * np.exp2(127.0 - byte)[:, None, :]).reshape(k, n).astype(np.float32)
    by_word = np.ascontiguousarray(scaled.reshape(k // 512, 128, 4, n).transpose(0, 1, 3, 2))
    if fmt == "e4m3":
        words = by_word.astype(ml_dtypes.float8_e4m3fn).view(np.uint8)
    else:
        c = by_word.astype(ml_dtypes.float4_e2m1fn).view(np.uint8) & 0xF
        words = c[..., 0::2] | (c[..., 1::2] << 4)
    return np.ascontiguousarray(words), np.ascontiguousarray(byte.astype(np.uint8).reshape(k // 512, 16, n))


def unpack_weight(words, scales, fmt):
    g, p, n, _ = words.shape
    if fmt == "e4m3":
        vals = np.ascontiguousarray(words).view(ml_dtypes.float8_e4m3fn).astype(np.float64)
    else:
        nib = np.empty((g, p, n, 4), np.uint8)
        nib[..., 0::2] = words & 0xF
        nib[..., 1::2] = words >> 4
        vals = E2M1[nib]
    vals = vals * np.repeat(np.exp2(scales.astype(np.float64) - 127.0), 8, axis=1)[..., None]
    return vals.transpose(0, 1, 3, 2).reshape(g * 512, n)


BQ, BK, L, H, DH = 4, 4, 512, 4, 128
D = H * DH
FMT = "e4m3"


def setup_inputs():
    s, t = mx_kscale(D), mx_kscale(D)
    amp_q = 0.5 + np.random.random((BQ, 1, 1))
    amp_k = 0.5 + np.random.random((BK, 1, 1))
    query_states = bf(np.random.standard_normal((BQ, L, D)) * amp_q * s)
    key_states = bf(np.random.standard_normal((BK, L, D)) * amp_k * s)
    Wq = np.random.standard_normal((D, D)) * 0.8 / np.sqrt(D) * t[:, None] / s[None, :]
    bq = bf(np.random.standard_normal(D) * 0.3 * t)
    Wk = np.random.standard_normal((D, D)) * 0.8 / np.sqrt(D) / t[:, None] / s[None, :]
    bk = bf(np.random.standard_normal(D) * 0.3 / t)
    logit_scale = bf(-1.5 + 0.1 * np.random.standard_normal(1))
    Wq_words, Wq_scales = pack_weight(np.ascontiguousarray(Wq.T), FMT)
    Wk_words, Wk_scales = pack_weight(np.ascontiguousarray(Wk.T), FMT)
    return {
        "query_states": query_states,
        "key_states": key_states,
        "Wq_words": Wq_words,
        "Wq_scales": Wq_scales,
        "bq": bq,
        "Wk_words": Wk_words,
        "Wk_scales": Wk_scales,
        "bk": bk,
        "logit_scale": logit_scale,
    }


def reference(query_states, key_states, Wq_words, Wq_scales, bq, Wk_words, Wk_scales, bk, logit_scale):
    q = (mxq(f64(query_states).reshape(BQ * L, D), 1, "e4m3") @ unpack_weight(Wq_words, Wq_scales, FMT)) + f64(bq)
    k = (mxq(f64(key_states).reshape(BK * L, D), 1, "e4m3") @ unpack_weight(Wk_words, Wk_scales, FMT)) + f64(bk)
    retrieve = mxq(q, 1, "e4m3") @ mxq(k, 1, "e4m3").T
    retrieve = retrieve.reshape(BQ, L, BK, L).transpose(0, 2, 1, 3)
    t2v = retrieve.max(axis=-1).sum(axis=2) / L
    v2t = retrieve.max(axis=-2).sum(axis=2) / L
    return np.exp(f64(logit_scale)) * (t2v + v2t) / 2.0

@@ -1,0 +1,195 @@
+from contextlib import ExitStack
+
+import concourse.mybir as mybir
+from concourse.masks import make_identity
+
+F32 = mybir.dt.float32
+BF16 = mybir.dt.bfloat16
+I32 = mybir.dt.int32
+U32 = mybir.dt.uint32
+U8 = mybir.dt.uint8
+FP8X4 = mybir.dt.float8_e4m3fn_x4
+ACT = mybir.ActivationFunctionType
+ALU = mybir.AluOpType
+AXIS_X = mybir.AxisListType.X
+
+P = 128
+PACK = 4
+SAMPLES = 4
+L = 512
+D = 512
+TILES = L // P
+QUADRANTS = 4
+
+FLOPS = 2 * 2 * SAMPLES * L * D * D + 2 * (SAMPLES * L) * (SAMPLES * L) * D
+
+
+def load_weight_codes(nc, pool, words, name):
+    codes = pool.tile([P, D], U32, name=name, align_bytes=64)
+    nc.sync.dma_start(out=codes[:].bitcast(I32), in_=words[0].rearrange("p n t -> p (n t)").bitcast(I32))
+    return codes
+
+
+def load_weight_scales(nc, pool, scale_rows, name):
+    plane = pool.tile([P, D], U8, name=name, align_bytes=64)
+    nc.vector.memset(plane[:].bitcast(I32), 0)
+    for quadrant in range(QUADRANTS):
+        nc.sync.dma_start(
+            out=plane[32 * quadrant : 32 * quadrant + 4, :].bitcast(I32),
+            in_=scale_rows[0, 4 * quadrant : 4 * quadrant + 4, :].bitcast(I32),
+        )
+    return plane
+
+
+def tile_attention_pa_kernel(
+    tc, query_states, key_states, Wq_words, Wq_scales, bq, Wk_words, Wk_scales, bk, logit_scale, out
+):
+    nc = tc.nc
+    with ExitStack() as pools:
+        const = pools.enter_context(tc.tile_pool(name="const", bufs=1))
+        inputs = pools.enter_context(tc.tile_pool(name="inputs", bufs=1))
+        work = pools.enter_context(tc.tile_pool(name="work", bufs=2))
+        keep = pools.enter_context(tc.tile_pool(name="keep", bufs=1))
+        psum_turn = pools.enter_context(tc.psum_pool(name="psum_turn", bufs=2))
+        psum_proj = pools.enter_context(tc.psum_pool(name="psum_proj", bufs=2))
+        psum_r = pools.enter_context(tc.psum_pool(name="psum_r", bufs=4))
+
+        states = {"k": key_states, "q": query_states}
+        order = [(side, s) for s in range(SAMPLES) for side in ("k", "q")]
+        x_in = {}
+        for side, s in order:
+            x_in[side, s] = inputs.tile([P, TILES, D], BF16, name="x_%s%d" % (side, s))
+
+        def load_sample(side, s):
+            nc.sync.dma_start(out=x_in[side, s][:], in_=states[side][s].rearrange("(p t) d -> p t d", t=TILES))
+
+        bias_rows = const.tile([P, P], BF16)
+        nc.vector.memset(bias_rows[:], 0.0)
+        nc.scalar.dma_start(out=bias_rows[0:TILES, :], in_=bk.rearrange("(j p) -> j p", p=P))
+        nc.scalar.dma_start(out=bias_rows[TILES : 2 * TILES, :], in_=bq.rearrange("(j p) -> j p", p=P))
+        log_gain = const.tile([1, 1], BF16)
+        nc.scalar.dma_start(out=log_gain[:], in_=logit_scale.rearrange("(o n) -> o n", o=1))
+
+        w_codes = {}
+        w_scales = {}
+        load_sample("k", 0)
+        w_codes["k"] = load_weight_codes(nc, const, Wk_words, "wk_codes")
+        load_sample("q", 0)
+        w_codes["q"] = load_weight_codes(nc, const, Wq_words, "wq_codes")
+        w_scales["k"] = load_weight_scales(nc, const, Wk_scales, "wk_scales")
+        w_scales["q"] = load_weight_scales(nc, const, Wq_scales, "wq_scales")
+        for side, s in order[2:]:
+            load_sample(side, s)
+
+        ident_f32 = const.tile([P, P], F32)
+        make_identity(nc, ident_f32[:])
+        ident_bf16 = const.tile([P, P], BF16)
+        make_identity(nc, ident_bf16[:])
+        mean_weights = const.tile([P, P], F32)
+        nc.vector.memset(mean_weights[:], 1.0 / (2 * L))
+        gain = const.tile([1, 1], F32)
+        nc.scalar.activation(out=gain[:], in_=log_gain[:], func=ACT.Exp)
+
+        bias_turned = psum_turn.tile([P, P], BF16, tag="turned")
+        nc.tensor.transpose(out=bias_turned[:], in_=bias_rows[:], identity=ident_bf16[:])
+        bias_cols = const.tile([P, 2 * TILES], F32)
+        nc.vector.tensor_copy(out=bias_cols[:], in_=bias_turned[:, 0 : 2 * TILES])
+        first_bias_col = {"k": 0, "q": TILES}
+
+        codes = {}
+        scales = {}
+        for side, s in order:
+            vector_helps = s == 0
+
+            x_words = x_in[side, s][:].bitcast(F32)
+            x_grouped = work.tile([P, L, PACK], BF16, align_bytes=64)
+            x_grouped_words = (
+                x_grouped[:]
+                .rearrange("p r t -> p (r t)")
+                .bitcast(F32)
+                .rearrange("p (h t r u) -> p h t r u", h=2, t=2, u=2)
+            )
+            for h in range(2):
+                turned = psum_turn.tile([P, 2, 2, P], F32, tag="turned")
+                for t in range(2):
+                    for u in range(2):
+                        nc.tensor.transpose(
+                            out=turned[:, t, u, :],
+                            in_=x_words[:, 2 * h + t, u : D // 2 : 2],
+                            identity=ident_f32[:],
+                        )
+                if vector_helps and h == 1:
+                    nc.vector.tensor_copy(out=x_grouped_words[:, h], in_=turned[:].rearrange("p t u r -> p t r u"))
+                else:
+                    nc.scalar.copy(out=x_grouped_words[:, h], in_=turned[:].rearrange("p t u r -> p t r u"))
+            x_codes = work.tile([P, L], U32, align_bytes=64)
+            x_scales = work.tile([P, L], U8, align_bytes=64)
+            nc.vector.quantize_mx(
+                out=x_codes[:].bitcast(FP8X4), scales=x_scales[:], in_=x_grouped[:].rearrange("p r t -> p (r t)")
+            )
+
+            planes = work.tile([P, TILES, L], BF16)
+            for j in range(TILES):
+                cols = slice(P * j, P * (j + 1))
+                projected = psum_proj.tile([P, L], F32)
+                nc.tensor.matmul_mx(
+                    out=projected[:],
+                    lhsT=w_codes[side][:, cols].bitcast(FP8X4),
+                    lhsT_scale=w_scales[side][:, cols],
+                    rhs=x_codes[:].bitcast(FP8X4),
+                    rhs_scale=x_scales[:],
+                    start=True,
+                    stop=True,
+                )
+                bias_col = first_bias_col[side] + j
+                bias = bias_cols[:, bias_col : bias_col + 1]
+                if vector_helps and j % 2 == 1:
+                    nc.vector.tensor_scalar_add(out=planes[:, j, :], in0=projected[:], scalar1=bias)
+                else:
+                    nc.scalar.activation(out=planes[:, j, :], in_=projected[:], func=ACT.Identity, bias=bias, scale=1.0)
+            grouped = work.tile([P, L, PACK], BF16, align_bytes=64)
+            grouped_runs = grouped[:].rearrange("p (c i) t -> p c t i", i=4)
+            planes_runs = planes[:].rearrange("p t (c i) -> p c t i", i=4)
+            if vector_helps:
+                nc.vector.tensor_copy(out=grouped_runs, in_=planes_runs)
+            else:
+                nc.scalar.copy(out=grouped_runs, in_=planes_runs)
+            codes[side, s] = keep.tile([P, L], U32, name="codes_%s%d" % (side, s), align_bytes=64)
+            scales[side, s] = keep.tile([P, L], U8, name="scales_%s%d" % (side, s), align_bytes=64)
+            nc.vector.quantize_mx(
+                out=codes[side, s][:].bitcast(FP8X4),
+                scales=scales[side, s][:],
+                in_=grouped[:].rearrange("p r t -> p (r t)"),
+            )
+
+        maxima = keep.tile([P, SAMPLES * SAMPLES, 2 * TILES], F32)
+        pairs = sorted([(a, b) for a in range(SAMPLES) for b in range(SAMPLES)], key=lambda ab: (max(ab), ab))
+        for a, b in pairs:
+            for way, (on_partitions, on_free) in enumerate(((("q", a), ("k", b)), (("k", b), ("q", a)))):
+                for t in range(TILES):
+                    cols = slice(P * t, P * (t + 1))
+                    r = psum_r.tile([P, L], F32)
+                    nc.tensor.matmul_mx(
+                        out=r[:],
+                        lhsT=codes[on_partitions][:, cols].bitcast(FP8X4),
+                        lhsT_scale=scales[on_partitions][:, cols],
+                        rhs=codes[on_free][:].bitcast(FP8X4),
+                        rhs_scale=scales[on_free][:],
+                        start=True,
+                        stop=True,
+                    )
+                    col = TILES * way + t
+                    nc.vector.tensor_reduce(
+                        out=maxima[:, SAMPLES * a + b, col : col + 1], in_=r[:], axis=AXIS_X, op=ALU.max
+                    )
+
+        partial = keep.tile([P, SAMPLES * SAMPLES], F32)
+        nc.vector.tensor_reduce(out=partial[:], in_=maxima[:], axis=AXIS_X, op=ALU.add)
+        means = psum_proj.tile([P, SAMPLES * SAMPLES], F32, tag="projected")
+        nc.tensor.matmul(out=means[:], lhsT=mean_weights[:], rhs=partial[:], start=True, stop=True)
+        half = SAMPLES * SAMPLES // 2
+        result = keep.tile([1, 2, 2 * half], F32)
+        nc.vector.tensor_scalar_mul(
+            out=result[:, :, 0:half], in0=means[0:1, :].rearrange("o (r c) -> o r c", r=2), scalar1=gain[:]
+        )
+        nc.sync.dma_start(out=out.rearrange("(o r a) b -> o r (a b)", o=1, r=2), in_=result[:, :, 0:half])

@@ -20,6 +20,8 @@ L = 512
 D = 512
 TILES = L // P
 QUADRANTS = 4
+FIRST_SHARED = 7
+N_SHARED = 4
 
 FLOPS = 2 * 2 * SAMPLES * L * D * D + 2 * (SAMPLES * L) * (SAMPLES * L) * D
 
@@ -41,6 +43,12 @@ def load_weight_scales(nc, pool, scale_rows, name):
     return plane
 
 
+def fold_into(nc, kept, other):
+    nc.gpsimd.tensor_sub(out=other, in0=other, in1=kept)
+    nc.scalar.activation(out=other, in_=other, func=ACT.Relu)
+    nc.gpsimd.tensor_add(out=kept, in0=kept, in1=other)
+
+
 def tile_attention_pa_kernel(
     tc, query_states, key_states, Wq_words, Wq_scales, bq, Wk_words, Wk_scales, bk, logit_scale, out
 ):
@@ -50,6 +58,7 @@ def tile_attention_pa_kernel(
         inputs = pools.enter_context(tc.tile_pool(name="inputs", bufs=1))
         work = pools.enter_context(tc.tile_pool(name="work", bufs=2))
         keep = pools.enter_context(tc.tile_pool(name="keep", bufs=1))
+        shared = pools.enter_context(tc.tile_pool(name="shared", bufs=N_SHARED))
         psum_turn = pools.enter_context(tc.psum_pool(name="psum_turn", bufs=2))
         psum_proj = pools.enter_context(tc.psum_pool(name="psum_proj", bufs=2))
         psum_r = pools.enter_context(tc.psum_pool(name="psum_r", bufs=4))
@@ -73,10 +82,10 @@ def tile_attention_pa_kernel(
         w_codes = {}
         w_scales = {}
         load_sample("k", 0)
-        w_codes["k"] = load_weight_codes(nc, const, Wk_words, "wk_codes")
         load_sample("q", 0)
-        w_codes["q"] = load_weight_codes(nc, const, Wq_words, "wq_codes")
+        w_codes["k"] = load_weight_codes(nc, const, Wk_words, "wk_codes")
         w_scales["k"] = load_weight_scales(nc, const, Wk_scales, "wk_scales")
+        w_codes["q"] = load_weight_codes(nc, const, Wq_words, "wq_codes")
         w_scales["q"] = load_weight_scales(nc, const, Wq_scales, "wq_scales")
         for side, s in order[2:]:
             load_sample(side, s)
@@ -164,24 +173,49 @@ def tile_attention_pa_kernel(
 
         maxima = keep.tile([P, SAMPLES * SAMPLES, 2 * TILES], F32)
         pairs = sorted([(a, b) for a in range(SAMPLES) for b in range(SAMPLES)], key=lambda ab: (max(ab), ab))
+        shared_pairs = pairs[FIRST_SHARED : FIRST_SHARED + N_SHARED]
+
+        def product_and_maxima(on_partitions, on_free, maxima_cols, copies):
+            for t in range(TILES):
+                cols = slice(P * t, P * (t + 1))
+                r = psum_r.tile([P, L], F32)
+                nc.tensor.matmul_mx(
+                    out=r[:],
+                    lhsT=codes[on_partitions][:, cols].bitcast(FP8X4),
+                    lhsT_scale=scales[on_partitions][:, cols],
+                    rhs=codes[on_free][:].bitcast(FP8X4),
+                    rhs_scale=scales[on_free][:],
+                    start=True,
+                    stop=True,
+                )
+                nc.vector.tensor_reduce(out=maxima_cols[:, t : t + 1], in_=r[:], axis=AXIS_X, op=ALU.max)
+                if copies is not None:
+                    nc.scalar.copy(out=copies[:, t, :], in_=r[:])
+
+        folded = {}
         for a, b in pairs:
-            for way, (on_partitions, on_free) in enumerate(((("q", a), ("k", b)), (("k", b), ("q", a)))):
-                for t in range(TILES):
-                    cols = slice(P * t, P * (t + 1))
-                    r = psum_r.tile([P, L], F32)
-                    nc.tensor.matmul_mx(
-                        out=r[:],
-                        lhsT=codes[on_partitions][:, cols].bitcast(FP8X4),
-                        lhsT_scale=scales[on_partitions][:, cols],
-                        rhs=codes[on_free][:].bitcast(FP8X4),
-                        rhs_scale=scales[on_free][:],
-                        start=True,
-                        stop=True,
-                    )
-                    col = TILES * way + t
-                    nc.vector.tensor_reduce(
-                        out=maxima[:, SAMPLES * a + b, col : col + 1], in_=r[:], axis=AXIS_X, op=ALU.max
-                    )
+            over_keys = maxima[:, SAMPLES * a + b, 0:TILES]
+            over_queries = maxima[:, SAMPLES * a + b, TILES : 2 * TILES]
+            if (a, b) not in shared_pairs:
+                product_and_maxima(("q", a), ("k", b), over_keys, None)
+                product_and_maxima(("k", b), ("q", a), over_queries, None)
+            else:
+                r_copies = shared.tile([P, TILES, L], F32)
+                product_and_maxima(("q", a), ("k", b), over_keys, r_copies)
+                fold_into(nc, r_copies[:, 0, :], r_copies[:, 1, :])
+                fold_into(nc, r_copies[:, 2, :], r_copies[:, 3, :])
+                fold_into(nc, r_copies[:, 0, :], r_copies[:, 2, :])
+                folded[a, b] = r_copies[:, 0, :]
+
+        for a, b in shared_pairs:
+            folded_turned = psum_turn.tile([P, TILES, P], F32, tag="turned")
+            for t in range(TILES):
+                nc.tensor.transpose(
+                    out=folded_turned[:, t, :], in_=folded[a, b][:, P * t : P * (t + 1)], identity=ident_f32[:]
+                )
+            nc.vector.tensor_reduce(
+                out=maxima[:, SAMPLES * a + b, TILES : 2 * TILES], in_=folded_turned[:], axis=AXIS_X, op=ALU.max
+            )
 
         partial = keep.tile([P, SAMPLES * SAMPLES], F32)
         nc.vector.tensor_reduce(out=partial[:], in_=maxima[:], axis=AXIS_X, op=ALU.add)

@@ -20,8 +20,6 @@ L = 512
 D = 512
 TILES = L // P
 QUADRANTS = 4
-FIRST_SHARED = 7
-N_SHARED = 4
 
 FLOPS = 2 * 2 * SAMPLES * L * D * D + 2 * (SAMPLES * L) * (SAMPLES * L) * D
 
@@ -43,12 +41,6 @@ def load_weight_scales(nc, pool, scale_rows, name):
     return plane
 
 
-def fold_into(nc, kept, other):
-    nc.gpsimd.tensor_sub(out=other, in0=other, in1=kept)
-    nc.scalar.activation(out=other, in_=other, func=ACT.Relu)
-    nc.gpsimd.tensor_add(out=kept, in0=kept, in1=other)
-
-
 def tile_attention_pa_kernel(
     tc, query_states, key_states, Wq_words, Wq_scales, bq, Wk_words, Wk_scales, bk, logit_scale, out
 ):
@@ -58,7 +50,6 @@ def tile_attention_pa_kernel(
         inputs = pools.enter_context(tc.tile_pool(name="inputs", bufs=1))
         work = pools.enter_context(tc.tile_pool(name="work", bufs=2))
         keep = pools.enter_context(tc.tile_pool(name="keep", bufs=1))
-        shared = pools.enter_context(tc.tile_pool(name="shared", bufs=N_SHARED))
         psum_turn = pools.enter_context(tc.psum_pool(name="psum_turn", bufs=2))
         psum_proj = pools.enter_context(tc.psum_pool(name="psum_proj", bufs=2))
         psum_r = pools.enter_context(tc.psum_pool(name="psum_r", bufs=4))
@@ -70,7 +61,9 @@ def tile_attention_pa_kernel(
             x_in[side, s] = inputs.tile([P, TILES, D], BF16, name="x_%s%d" % (side, s))
 
         def load_sample(side, s):
-            nc.sync.dma_start(out=x_in[side, s][:], in_=states[side][s].rearrange("(p t) d -> p t d", t=TILES))
+            rows = states[side][s].rearrange("(p t) d -> p t d", t=TILES)
+            for h in range(2):
+                nc.sync.dma_start(out=x_in[side, s][:, 2 * h : 2 * h + 2, :], in_=rows[:, 2 * h : 2 * h + 2, :])
 
         bias_rows = const.tile([P, P], BF16)
         nc.vector.memset(bias_rows[:], 0.0)
@@ -108,7 +101,7 @@ def tile_attention_pa_kernel(
         codes = {}
         scales = {}
         for side, s in order:
-            vector_helps = s == 0
+            on_vector = s == 0
 
             x_words = x_in[side, s][:].bitcast(F32)
             x_grouped = work.tile([P, L, PACK], BF16, align_bytes=64)
@@ -127,42 +120,52 @@ def tile_attention_pa_kernel(
                             in_=x_words[:, 2 * h + t, u : D // 2 : 2],
                             identity=ident_f32[:],
                         )
-                if vector_helps and h == 1:
-                    nc.vector.tensor_copy(out=x_grouped_words[:, h], in_=turned[:].rearrange("p t u r -> p t r u"))
-                else:
-                    nc.scalar.copy(out=x_grouped_words[:, h], in_=turned[:].rearrange("p t u r -> p t r u"))
+                nc.scalar.copy(out=x_grouped_words[:, h], in_=turned[:].rearrange("p t u r -> p t r u"))
             x_codes = work.tile([P, L], U32, align_bytes=64)
             x_scales = work.tile([P, L], U8, align_bytes=64)
             nc.vector.quantize_mx(
                 out=x_codes[:].bitcast(FP8X4), scales=x_scales[:], in_=x_grouped[:].rearrange("p r t -> p (r t)")
             )
 
-            planes = work.tile([P, TILES, L], BF16)
-            for j in range(TILES):
+            grouped = work.tile([P, L, PACK], BF16, align_bytes=64)
+            bias = bias_cols[:, first_bias_col[side] : first_bias_col[side] + TILES]
+
+            def project(bank, j, tokens):
                 cols = slice(P * j, P * (j + 1))
-                projected = psum_proj.tile([P, L], F32)
                 nc.tensor.matmul_mx(
-                    out=projected[:],
+                    out=bank,
                     lhsT=w_codes[side][:, cols].bitcast(FP8X4),
                     lhsT_scale=w_scales[side][:, cols],
-                    rhs=x_codes[:].bitcast(FP8X4),
-                    rhs_scale=x_scales[:],
+                    rhs=x_codes[:, tokens].bitcast(FP8X4),
+                    rhs_scale=x_scales[:, tokens],
                     start=True,
                     stop=True,
                 )
-                bias_col = first_bias_col[side] + j
-                bias = bias_cols[:, bias_col : bias_col + 1]
-                if vector_helps and j % 2 == 1:
-                    nc.vector.tensor_scalar_add(out=planes[:, j, :], in0=projected[:], scalar1=bias)
-                else:
-                    nc.scalar.activation(out=planes[:, j, :], in_=projected[:], func=ACT.Identity, bias=bias, scale=1.0)
-            grouped = work.tile([P, L, PACK], BF16, align_bytes=64)
-            grouped_runs = grouped[:].rearrange("p (c i) t -> p c t i", i=4)
-            planes_runs = planes[:].rearrange("p t (c i) -> p c t i", i=4)
-            if vector_helps:
-                nc.vector.tensor_copy(out=grouped_runs, in_=planes_runs)
+
+            if on_vector:
+                for c in range(TILES):
+                    tokens = slice(P * c, P * (c + 1))
+                    projected = psum_proj.tile([P, TILES, P], F32, tag="projected")
+                    for j in range(TILES):
+                        project(projected[:, j, :], j, tokens)
+                    nc.vector.tensor_tensor(
+                        out=grouped[:, tokens, :],
+                        in0=projected[:].rearrange("p j r -> p r j"),
+                        in1=bias.unsqueeze(1).to_broadcast([P, P, PACK]),
+                        op=ALU.add,
+                    )
             else:
-                nc.scalar.copy(out=grouped_runs, in_=planes_runs)
+                planes = work.tile([P, TILES, L], BF16)
+                for j in range(TILES):
+                    projected = psum_proj.tile([P, L], F32, tag="projected")
+                    project(projected[:], j, slice(0, L))
+                    nc.scalar.activation(
+                        out=planes[:, j, :], in_=projected[:], func=ACT.Identity, bias=bias[:, j : j + 1], scale=1.0
+                    )
+                nc.scalar.copy(
+                    out=grouped[:].rearrange("p (c i) t -> p c t i", i=4),
+                    in_=planes[:].rearrange("p t (c i) -> p c t i", i=4),
+                )
             codes[side, s] = keep.tile([P, L], U32, name="codes_%s%d" % (side, s), align_bytes=64)
             scales[side, s] = keep.tile([P, L], U8, name="scales_%s%d" % (side, s), align_bytes=64)
             nc.vector.quantize_mx(
@@ -173,49 +176,25 @@ def tile_attention_pa_kernel(
 
         maxima = keep.tile([P, SAMPLES * SAMPLES, 2 * TILES], F32)
         pairs = sorted([(a, b) for a in range(SAMPLES) for b in range(SAMPLES)], key=lambda ab: (max(ab), ab))
-        shared_pairs = pairs[FIRST_SHARED : FIRST_SHARED + N_SHARED]
-
-        def product_and_maxima(on_partitions, on_free, maxima_cols, copies):
-            for t in range(TILES):
-                cols = slice(P * t, P * (t + 1))
-                r = psum_r.tile([P, L], F32)
-                nc.tensor.matmul_mx(
-                    out=r[:],
-                    lhsT=codes[on_partitions][:, cols].bitcast(FP8X4),
-                    lhsT_scale=scales[on_partitions][:, cols],
-                    rhs=codes[on_free][:].bitcast(FP8X4),
-                    rhs_scale=scales[on_free][:],
-                    start=True,
-                    stop=True,
-                )
-                nc.vector.tensor_reduce(out=maxima_cols[:, t : t + 1], in_=r[:], axis=AXIS_X, op=ALU.max)
-                if copies is not None:
-                    nc.scalar.copy(out=copies[:, t, :], in_=r[:])
-
-        folded = {}
         for a, b in pairs:
-            over_keys = maxima[:, SAMPLES * a + b, 0:TILES]
-            over_queries = maxima[:, SAMPLES * a + b, TILES : 2 * TILES]
-            if (a, b) not in shared_pairs:
-                product_and_maxima(("q", a), ("k", b), over_keys, None)
-                product_and_maxima(("k", b), ("q", a), over_queries, None)
-            else:
-                r_copies = shared.tile([P, TILES, L], F32)
-                product_and_maxima(("q", a), ("k", b), over_keys, r_copies)
-                fold_into(nc, r_copies[:, 0, :], r_copies[:, 1, :])
-                fold_into(nc, r_copies[:, 2, :], r_copies[:, 3, :])
-                fold_into(nc, r_copies[:, 0, :], r_copies[:, 2, :])
-                folded[a, b] = r_copies[:, 0, :]
-
-        for a, b in shared_pairs:
-            folded_turned = psum_turn.tile([P, TILES, P], F32, tag="turned")
-            for t in range(TILES):
-                nc.tensor.transpose(
-                    out=folded_turned[:, t, :], in_=folded[a, b][:, P * t : P * (t + 1)], identity=ident_f32[:]
-                )
-            nc.vector.tensor_reduce(
-                out=maxima[:, SAMPLES * a + b, TILES : 2 * TILES], in_=folded_turned[:], axis=AXIS_X, op=ALU.max
-            )
+            for way, (on_partitions, on_free) in enumerate(((("q", a), ("k", b)), (("k", b), ("q", a)))):
+                for t in range(TILES):
+                    cols = slice(P * t, P * (t + 1))
+                    r = psum_r.tile([P, L], F32)
+                    with tc.high_priority():
+                        nc.tensor.matmul_mx(
+                            out=r[:],
+                            lhsT=codes[on_partitions][:, cols].bitcast(FP8X4),
+                            lhsT_scale=scales[on_partitions][:, cols],
+                            rhs=codes[on_free][:].bitcast(FP8X4),
+                            rhs_scale=scales[on_free][:],
+                            start=True,
+                            stop=True,
+                        )
+                    col = TILES * way + t
+                    nc.vector.tensor_reduce(
+                        out=maxima[:, SAMPLES * a + b, col : col + 1], in_=r[:], axis=AXIS_X, op=ALU.max
+                    )
 
         partial = keep.tile([P, SAMPLES * SAMPLES], F32)
         nc.vector.tensor_reduce(out=partial[:], in_=maxima[:], axis=AXIS_X, op=ALU.add)

@@ -21,7 +21,25 @@ D = 512
 TILES = L // P
 QUADRANTS = 4
 
+HALF = L // 2
+HALVES = (slice(0, HALF), slice(HALF, L))
+WHOLE = slice(0, L)
 FLOPS = 2 * 2 * SAMPLES * L * D * D + 2 * (SAMPLES * L) * (SAMPLES * L) * D
+BY_VECTOR = []
+BY_GPSIMD = []
+OFFSET = {"turn": -32, "quantize_input": -26, "leave": -18, "interleave": -10, "quantize": -3, "negate": -5, "quantize_negative": -2}
+FIRST_FOLDED = 2
+LEAVE_STEP = 3
+TURN_STEP = 1
+IL_STEP = 1
+NEG0 = 8
+AHEAD = 2
+AHEAD_PREP = 0
+FINISH_LAG = 8
+FINISH_GAP = 0
+LAST_DIRECT = 0
+HALVE_AT = [2, 3]
+WARM_UP = 0
 
 
 def load_weight_codes(nc, pool, words, name):
@@ -48,11 +66,12 @@ def tile_attention_pa_kernel(
     with ExitStack() as pools:
         const = pools.enter_context(tc.tile_pool(name="const", bufs=1))
         inputs = pools.enter_context(tc.tile_pool(name="inputs", bufs=1))
-        work = pools.enter_context(tc.tile_pool(name="work", bufs=2))
+        work = pools.enter_context(tc.tile_pool(name="work", bufs=3))
         keep = pools.enter_context(tc.tile_pool(name="keep", bufs=1))
-        psum_turn = pools.enter_context(tc.psum_pool(name="psum_turn", bufs=2))
-        psum_proj = pools.enter_context(tc.psum_pool(name="psum_proj", bufs=2))
-        psum_r = pools.enter_context(tc.psum_pool(name="psum_r", bufs=4))
+        fold = pools.enter_context(tc.tile_pool(name="fold", bufs=6))
+        psum_v = pools.enter_context(tc.psum_pool(name="psum_v", bufs=4))
+        psum_s = pools.enter_context(tc.psum_pool(name="psum_s", bufs=4))
+        pools.enter_context(tc.manual_schedule())
 
         states = {"k": key_states, "q": query_states}
         order = [(side, s) for s in range(SAMPLES) for side in ("k", "q")]
@@ -65,16 +84,13 @@ def tile_attention_pa_kernel(
             for h in range(2):
                 nc.sync.dma_start(out=x_in[side, s][:, 2 * h : 2 * h + 2, :], in_=rows[:, 2 * h : 2 * h + 2, :])
 
-        bias_rows = const.tile([P, P], BF16)
-        nc.vector.memset(bias_rows[:], 0.0)
-        nc.scalar.dma_start(out=bias_rows[0:TILES, :], in_=bk.rearrange("(j p) -> j p", p=P))
-        nc.scalar.dma_start(out=bias_rows[TILES : 2 * TILES, :], in_=bq.rearrange("(j p) -> j p", p=P))
-        log_gain = const.tile([1, 1], BF16)
-        nc.scalar.dma_start(out=log_gain[:], in_=logit_scale.rearrange("(o n) -> o n", o=1))
-
         w_codes = {}
         w_scales = {}
         load_sample("k", 0)
+        bias_rows = const.tile([P, P], BF16)
+        nc.vector.memset(bias_rows[:], 0.0)
+        nc.sync.dma_start(out=bias_rows[0:TILES, :], in_=bk.rearrange("(j p) -> j p", p=P))
+        nc.sync.dma_start(out=bias_rows[TILES : 2 * TILES, :], in_=bq.rearrange("(j p) -> j p", p=P))
         load_sample("q", 0)
         w_codes["k"] = load_weight_codes(nc, const, Wk_words, "wk_codes")
         w_scales["k"] = load_weight_scales(nc, const, Wk_scales, "wk_scales")
@@ -82,127 +98,296 @@ def tile_attention_pa_kernel(
         w_scales["q"] = load_weight_scales(nc, const, Wq_scales, "wq_scales")
         for side, s in order[2:]:
             load_sample(side, s)
+        log_gain = const.tile([P, 1], BF16)
+        nc.sync.dma_start(out=log_gain[:], in_=logit_scale.partition_broadcast(P))
 
         ident_f32 = const.tile([P, P], F32)
         make_identity(nc, ident_f32[:])
         ident_bf16 = const.tile([P, P], BF16)
         make_identity(nc, ident_bf16[:])
-        mean_weights = const.tile([P, P], F32)
-        nc.vector.memset(mean_weights[:], 1.0 / (2 * L))
-        gain = const.tile([1, 1], F32)
-        nc.scalar.activation(out=gain[:], in_=log_gain[:], func=ACT.Exp)
+        mean = const.tile([P, P], F32)
+        nc.gpsimd.memset(mean[:], 1.0 / (2 * L))
+        warm = const.tile([1, 1], F32)
+        nc.vector.memset(warm[:], 0.0)
+        nc.scalar.activation(out=warm[:], in_=warm[:], func=ACT.Exp)
 
-        bias_turned = psum_turn.tile([P, P], BF16, tag="turned")
-        nc.tensor.transpose(out=bias_turned[:], in_=bias_rows[:], identity=ident_bf16[:])
-        bias_cols = const.tile([P, 2 * TILES], F32)
-        nc.vector.tensor_copy(out=bias_cols[:], in_=bias_turned[:, 0 : 2 * TILES])
-        first_bias_col = {"k": 0, "q": TILES}
-
+        x_grouped = {}
+        x_codes = {}
+        x_scales = {}
+        planes = {}
+        grouped = {}
         codes = {}
         scales = {}
-        for side, s in order:
-            on_vector = s == 0
+        grouped_neg = {}
+        neg_codes = {}
+        neg_scales = {}
+        bias_cols = const.tile([P, 2 * TILES], F32)
 
+        def bias(side):
+            first = {"k": 0, "q": TILES}[side]
+            return bias_cols[:, first : first + TILES]
+
+        def turn(side, s, h):
             x_words = x_in[side, s][:].bitcast(F32)
-            x_grouped = work.tile([P, L, PACK], BF16, align_bytes=64)
+            if h == 0:
+                x_grouped[side, s] = work.tile([P, L, PACK], BF16, name="x_grouped", align_bytes=64)
             x_grouped_words = (
-                x_grouped[:]
+                x_grouped[side, s][:]
                 .rearrange("p r t -> p (r t)")
                 .bitcast(F32)
                 .rearrange("p (h t r u) -> p h t r u", h=2, t=2, u=2)
             )
-            for h in range(2):
-                turned = psum_turn.tile([P, 2, 2, P], F32, tag="turned")
-                for t in range(2):
-                    for u in range(2):
-                        nc.tensor.transpose(
-                            out=turned[:, t, u, :],
-                            in_=x_words[:, 2 * h + t, u : D // 2 : 2],
-                            identity=ident_f32[:],
-                        )
-                nc.scalar.copy(out=x_grouped_words[:, h], in_=turned[:].rearrange("p t u r -> p t r u"))
-            x_codes = work.tile([P, L], U32, align_bytes=64)
-            x_scales = work.tile([P, L], U8, align_bytes=64)
+            turned = psum_s.tile([P, 2, 2, P], F32, name="turned", tag="s")
+            for t in range(2):
+                for u in range(2):
+                    nc.tensor.transpose(
+                        out=turned[:, t, u, :],
+                        in_=x_words[:, 2 * h + t, u : D // 2 : 2],
+                        identity=ident_f32[:],
+                    )
+            nc.scalar.copy(out=x_grouped_words[:, h], in_=turned[:].rearrange("p t u r -> p t r u"))
+
+        def quantize_input(side, s):
+            x_codes[side, s] = work.tile([P, L], U32, name="x_codes", align_bytes=64)
+            x_scales[side, s] = work.tile([P, L], U8, name="x_scales", align_bytes=64)
             nc.vector.quantize_mx(
-                out=x_codes[:].bitcast(FP8X4), scales=x_scales[:], in_=x_grouped[:].rearrange("p r t -> p (r t)")
+                out=x_codes[side, s][:].bitcast(FP8X4),
+                scales=x_scales[side, s][:],
+                in_=x_grouped[side, s][:].rearrange("p r t -> p (r t)"),
             )
 
-            grouped = work.tile([P, L, PACK], BF16, align_bytes=64)
-            bias = bias_cols[:, first_bias_col[side] : first_bias_col[side] + TILES]
+        def project(side, s, bank, j, tokens):
+            cols = slice(P * j, P * (j + 1))
+            nc.tensor.matmul_mx(
+                out=bank,
+                lhsT=w_codes[side][:, cols].bitcast(FP8X4),
+                lhsT_scale=w_scales[side][:, cols],
+                rhs=x_codes[side, s][:, tokens].bitcast(FP8X4),
+                rhs_scale=x_scales[side, s][:, tokens],
+                start=True,
+                stop=True,
+            )
 
-            def project(bank, j, tokens):
-                cols = slice(P * j, P * (j + 1))
-                nc.tensor.matmul_mx(
-                    out=bank,
-                    lhsT=w_codes[side][:, cols].bitcast(FP8X4),
-                    lhsT_scale=w_scales[side][:, cols],
-                    rhs=x_codes[:, tokens].bitcast(FP8X4),
-                    rhs_scale=x_scales[:, tokens],
-                    start=True,
-                    stop=True,
-                )
+        def leave_by_vector(side, s, c):
+            if c == 0:
+                grouped[side, s] = work.tile([P, L, PACK], BF16, name="grouped", align_bytes=64)
+            tokens = slice(P * c, P * (c + 1))
+            projected = psum_v.tile([P, TILES, P], F32, name="projected", tag="v")
+            for j in range(TILES):
+                project(side, s, projected[:, j, :], j, tokens)
+            nc.vector.tensor_tensor(
+                out=grouped[side, s][:, tokens, :],
+                in0=projected[:].rearrange("p j r -> p r j"),
+                in1=bias(side).unsqueeze(1).to_broadcast([P, P, PACK]),
+                op=ALU.add,
+            )
 
-            if on_vector:
-                for c in range(TILES):
-                    tokens = slice(P * c, P * (c + 1))
-                    projected = psum_proj.tile([P, TILES, P], F32, tag="projected")
-                    for j in range(TILES):
-                        project(projected[:, j, :], j, tokens)
-                    nc.vector.tensor_tensor(
-                        out=grouped[:, tokens, :],
-                        in0=projected[:].rearrange("p j r -> p r j"),
-                        in1=bias.unsqueeze(1).to_broadcast([P, P, PACK]),
-                        op=ALU.add,
-                    )
-            else:
-                planes = work.tile([P, TILES, L], BF16)
-                for j in range(TILES):
-                    projected = psum_proj.tile([P, L], F32, tag="projected")
-                    project(projected[:], j, slice(0, L))
-                    nc.scalar.activation(
-                        out=planes[:, j, :], in_=projected[:], func=ACT.Identity, bias=bias[:, j : j + 1], scale=1.0
-                    )
-                nc.scalar.copy(
-                    out=grouped[:].rearrange("p (c i) t -> p c t i", i=4),
-                    in_=planes[:].rearrange("p t (c i) -> p c t i", i=4),
-                )
-            codes[side, s] = keep.tile([P, L], U32, name="codes_%s%d" % (side, s), align_bytes=64)
-            scales[side, s] = keep.tile([P, L], U8, name="scales_%s%d" % (side, s), align_bytes=64)
+        def leave_by_scalar(side, s, j, tokens):
+            if (side, s) not in planes:
+                planes[side, s] = work.tile([P, TILES, L], BF16, name="planes")
+            projected = psum_s.tile([P, tokens.stop - tokens.start], F32, name="projected", tag="s")
+            project(side, s, projected[:], j, tokens)
+            nc.scalar.activation(
+                out=planes[side, s][:, j, tokens],
+                in_=projected[:],
+                func=ACT.Identity,
+                bias=bias(side)[:, j : j + 1],
+                scale=1.0,
+            )
+
+        def interleave(side, s, h, copy):
+            if h == 0:
+                grouped[side, s] = work.tile([P, L, PACK], BF16, name="grouped", align_bytes=64)
+            tokens = HALVES[h]
+            copy(
+                out=grouped[side, s][:, tokens, :].rearrange("p (c i) t -> p c t i", i=4),
+                in_=planes[side, s][:, :, tokens].rearrange("p t (c i) -> p c t i", i=4),
+            )
+
+        def quantize(side, s, tokens):
+            if (side, s) not in codes:
+                codes[side, s] = keep.tile([P, L], U32, name="codes_%s%d" % (side, s), align_bytes=64)
+                scales[side, s] = keep.tile([P, L], U8, name="scales_%s%d" % (side, s), align_bytes=64)
             nc.vector.quantize_mx(
-                out=codes[side, s][:].bitcast(FP8X4),
-                scales=scales[side, s][:],
-                in_=grouped[:].rearrange("p r t -> p (r t)"),
+                out=codes[side, s][:, tokens].bitcast(FP8X4),
+                scales=scales[side, s][:, tokens],
+                in_=grouped[side, s][:, tokens, :].rearrange("p r t -> p (r t)"),
+            )
+
+        def negate(s):
+            grouped_neg[s] = work.tile([P, HALF, PACK], BF16, name="grouped_neg", align_bytes=64)
+            nc.gpsimd.tensor_scalar(
+                out=grouped_neg[s][:],
+                in0=grouped["q", s][:, HALVES[0], :],
+                scalar1=-1.0,
+                scalar2=0.0,
+                op0=ALU.mult,
+                op1=ALU.add,
+            )
+
+        def quantize_negative(s):
+            neg_codes[s] = keep.tile([P, HALF], U32, name="neg_codes_%d" % s, align_bytes=64)
+            neg_scales[s] = keep.tile([P, HALF], U8, name="neg_scales_%d" % s, align_bytes=64)
+            nc.vector.quantize_mx(
+                out=neg_codes[s][:].bitcast(FP8X4),
+                scales=neg_scales[s][:],
+                in_=grouped_neg[s][:].rearrange("p r t -> p (r t)"),
             )
 
         maxima = keep.tile([P, SAMPLES * SAMPLES, 2 * TILES], F32)
-        pairs = sorted([(a, b) for a in range(SAMPLES) for b in range(SAMPLES)], key=lambda ab: (max(ab), ab))
-        for a, b in pairs:
-            for way, (on_partitions, on_free) in enumerate(((("q", a), ("k", b)), (("k", b), ("q", a)))):
-                for t in range(TILES):
-                    cols = slice(P * t, P * (t + 1))
-                    r = psum_r.tile([P, L], F32)
-                    with tc.high_priority():
-                        nc.tensor.matmul_mx(
-                            out=r[:],
-                            lhsT=codes[on_partitions][:, cols].bitcast(FP8X4),
-                            lhsT_scale=scales[on_partitions][:, cols],
-                            rhs=codes[on_free][:].bitcast(FP8X4),
-                            rhs_scale=scales[on_free][:],
-                            start=True,
-                            stop=True,
-                        )
-                    col = TILES * way + t
-                    nc.vector.tensor_reduce(
-                        out=maxima[:, SAMPLES * a + b, col : col + 1], in_=r[:], axis=AXIS_X, op=ALU.max
-                    )
+        tops = {}
 
-        partial = keep.tile([P, SAMPLES * SAMPLES], F32)
-        nc.vector.tensor_reduce(out=partial[:], in_=maxima[:], axis=AXIS_X, op=ALU.add)
-        means = psum_proj.tile([P, SAMPLES * SAMPLES], F32, tag="projected")
-        nc.tensor.matmul(out=means[:], lhsT=mean_weights[:], rhs=partial[:], start=True, stop=True)
+        def product(bank, stationary, t, moving, moving_scales, start, stop):
+            cols = slice(P * t, P * (t + 1))
+            nc.tensor.matmul_mx(
+                out=bank,
+                lhsT=codes[stationary][:, cols].bitcast(FP8X4),
+                lhsT_scale=scales[stationary][:, cols],
+                rhs=moving.bitcast(FP8X4),
+                rhs_scale=moving_scales,
+                start=start,
+                stop=stop,
+            )
+
+        def direct(on_partitions, on_free, t, out_col):
+            r = psum_v.tile([P, L], F32, name="r", tag="v")
+            product(r[:], on_partitions, t, codes[on_free][:], scales[on_free][:], True, True)
+            return lambda: nc.vector.tensor_reduce(out=out_col, in_=r[:], axis=AXIS_X, op=ALU.max)
+
+        def halve(a, b, two):
+            first = psum_s.tile([P, 2, HALF], F32, name="first", tag="s")
+            for i in range(2):
+                low = HALVES[0]
+                product(first[:, i, :], ("k", b), 2 * two + i, codes["q", a][:, low], scales["q", a][:, low], True, True)
+            base = fold.tile([P, 2, HALF], F32, name="base")
+            nc.scalar.copy(out=base[:], in_=first[:])
+            step = psum_s.tile([P, 2, HALF], F32, name="step", tag="s")
+            for i in range(2):
+                high = HALVES[1]
+                product(step[:, i, :], ("k", b), 2 * two + i, codes["q", a][:, high], scales["q", a][:, high], True, False)
+                product(step[:, i, :], ("k", b), 2 * two + i, neg_codes[a][:], neg_scales[a][:], False, True)
+            rise = fold.tile([P, 2, HALF], F32, name="rise")
+            nc.scalar.activation(out=rise[:], in_=step[:], func=ACT.Relu)
+            tops[a, b, two] = fold.tile([P, 2, HALF], F32, name="top")
+            nc.gpsimd.tensor_tensor(out=tops[a, b, two][:], in0=base[:], in1=rise[:], op=ALU.add)
+            return lambda: None
+
+        def finish(a, b, two, out_cols):
+            return lambda: nc.vector.tensor_reduce(out=out_cols, in_=tops[a, b, two][:], axis=AXIS_X, op=ALU.max)
+
+        for h in range(2):
+            turn("k", 0, h)
+        bias_turned = psum_s.tile([P, P], BF16, name="bias_turned", tag="s")
+        nc.tensor.transpose(out=bias_turned[:], in_=bias_rows[:], identity=ident_bf16[:])
+        nc.vector.tensor_copy(out=bias_cols[:], in_=bias_turned[:, 0 : 2 * TILES])
+        quantize_input("k", 0)
+        for h in range(2):
+            turn("q", 0, h)
+        quantize_input("q", 0)
+        for c in range(TILES):
+            leave_by_vector("k", 0, c)
+        for h in range(2):
+            for j in range(TILES):
+                leave_by_scalar("q", 0, j, HALVES[h])
+        interleave("q", 0, 0, nc.vector.tensor_copy)
+        quantize("k", 0, WHOLE)
+        quantize("q", 0, HALVES[0])
+        interleave("q", 0, 1, nc.vector.tensor_copy)
+        for h in range(2):
+            turn("k", 1, h)
+        quantize_input("k", 1)
+        quantize("q", 0, HALVES[1])
+        for j in range(TILES):
+            leave_by_scalar("k", 1, j, WHOLE)
+
+        ready = {sample: n for n, sample in enumerate(order)}
+        pairs = sorted(
+            [(a, b) for a in range(SAMPLES) for b in range(SAMPLES)],
+            key=lambda ab: (max(ready["q", ab[0]], ready["k", ab[1]]), ab),
+        )
+        items = []
+        late = []
+        first_use = {}
+        for n, (a, b) in enumerate(pairs):
+            row = maxima[:, SAMPLES * a + b, :]
+            for sample in (("q", a), ("k", b)):
+                first_use.setdefault(sample, len(items))
+            if FIRST_FOLDED <= n < len(pairs) - LAST_DIRECT:
+                for t in range(TILES):
+                    items.append((direct, (("q", a), ("k", b), t, row[:, t : t + 1])))
+                    if t in HALVE_AT:
+                        items.append((halve, (a, b, HALVE_AT.index(t))))
+                late.append((len(items) + FINISH_LAG, finish, (a, b, 0, row[:, TILES : TILES + 2])))
+                late.append((len(items) + FINISH_LAG + FINISH_GAP, finish, (a, b, 1, row[:, TILES + 2 : 2 * TILES])))
+            else:
+                for t in range(TILES):
+                    items.append((direct, (("q", a), ("k", b), t, row[:, t : t + 1])))
+                for t in range(TILES):
+                    col = TILES + t
+                    items.append((direct, (("k", b), ("q", a), t, row[:, col : col + 1])))
+            while late and late[0][0] <= len(items):
+                items.append(late.pop(0)[1:])
+        items += [entry[1:] for entry in late]
+
+        def by_gpsimd(out, in_):
+            nc.gpsimd.tensor_scalar(out=out, in0=in_, scalar1=1.0, scalar2=0.0, op0=ALU.mult, op1=ALU.add)
+
+        due = {}
+
+        def plan(n, stage, arguments):
+            due.setdefault(n, []).append((stage, arguments))
+
+        for sample in order[1:]:
+            use = first_use[sample]
+            if sample[0] == "q":
+                plan(use + OFFSET["negate"] if sample[1] > 0 else NEG0, negate, sample[1:])
+                plan(use + OFFSET["quantize_negative"] if sample[1] > 0 else NEG0 + 4, quantize_negative, sample[1:])
+        for sample in order[2:]:
+            use = first_use[sample]
+            copy = nc.vector.tensor_copy if sample in BY_VECTOR else by_gpsimd if sample in BY_GPSIMD else nc.scalar.copy
+            if sample != order[2]:
+                for h in range(2):
+                    plan(use + OFFSET["turn"] + TURN_STEP * h, turn, sample + (h,))
+                plan(use + OFFSET["quantize_input"], quantize_input, sample)
+                for j in range(TILES):
+                    plan(use + OFFSET["leave"] + LEAVE_STEP * j // 2, leave_by_scalar, sample + (j, WHOLE))
+            for h in range(2):
+                plan(use + OFFSET["interleave"] + IL_STEP * h, interleave, sample + (h, copy))
+            plan(use + OFFSET["quantize"], quantize, sample + (WHOLE,))
+
+        consumers = []
+        for n in range(len(items) + AHEAD):
+            for at in sorted(due):
+                if at <= n - AHEAD_PREP:
+                    for stage, arguments in due.pop(at):
+                        stage(*arguments)
+            if n >= AHEAD:
+                consumers[n - AHEAD]()
+            if n < len(items):
+                stage, arguments = items[n]
+                consumers.append(stage(*arguments))
+            if n == 0:
+                gain = const.tile([P, 1], F32)
+                nc.scalar.activation(out=gain[:], in_=log_gain[:], func=ACT.Exp)
+                mean_weights = const.tile([P, P], F32)
+                nc.gpsimd.tensor_scalar(
+                    out=mean_weights[:], in0=mean[:], scalar1=gain[:], scalar2=0.0, op0=ALU.mult, op1=ALU.add
+                )
+
+        sums = psum_v.tile([P, SAMPLES * SAMPLES, 2 * TILES], F32, name="sums", tag="v")
+        nc.tensor.matmul(
+            out=sums[:].rearrange("p n c -> p (n c)"),
+            lhsT=mean_weights[:],
+            rhs=maxima[:].rearrange("p n c -> p (n c)"),
+            start=True,
+            stop=True,
+        )
         half = SAMPLES * SAMPLES // 2
         result = keep.tile([1, 2, 2 * half], F32)
-        nc.vector.tensor_scalar_mul(
-            out=result[:, :, 0:half], in0=means[0:1, :].rearrange("o (r c) -> o r c", r=2), scalar1=gain[:]
+        nc.vector.tensor_reduce(
+            out=result[:, :, 0:half],
+            in_=sums[0:1, :, :].rearrange("o (r n) c -> o r n c", r=2),
+            axis=AXIS_X,
+            op=ALU.add,
         )
         nc.sync.dma_start(out=out.rearrange("(o r a) b -> o r (a b)", o=1, r=2), in_=result[:, :, 0:half])

@@ -30,6 +30,10 @@ BY_GPSIMD = []
 OFFSET = {"turn": -32, "quantize_input": -26, "leave": -18, "interleave": -10, "quantize": -3, "negate": -5, "quantize_negative": -2}
 FIRST_FOLDED = 2
 LEAVE_STEP = 3
+THIRD = lambda n: False
+MIN_QI = 0
+MIN_LEAVE = 2
+MIN_Q = 3
 TURN_STEP = 1
 IL_STEP = 1
 NEG0 = 8
@@ -237,43 +241,52 @@ def tile_attention_pa_kernel(
         maxima = keep.tile([P, SAMPLES * SAMPLES, 2 * TILES], F32)
         tops = {}
 
-        def product(bank, stationary, t, moving, moving_scales, start, stop):
-            cols = slice(P * t, P * (t + 1))
+        def part(sample, cols):
+            return codes[sample][:, cols], scales[sample][:, cols]
+
+        def negative(s, cols):
+            return neg_codes[s][:, cols], neg_scales[s][:, cols]
+
+        def multiply(bank, stationary, moving, start, stop):
             nc.tensor.matmul_mx(
                 out=bank,
-                lhsT=codes[stationary][:, cols].bitcast(FP8X4),
-                lhsT_scale=scales[stationary][:, cols],
-                rhs=moving.bitcast(FP8X4),
-                rhs_scale=moving_scales,
+                lhsT=stationary[0].bitcast(FP8X4),
+                lhsT_scale=stationary[1],
+                rhs=moving[0].bitcast(FP8X4),
+                rhs_scale=moving[1],
                 start=start,
                 stop=stop,
             )
 
         def direct(on_partitions, on_free, t, out_col):
             r = psum_v.tile([P, L], F32, name="r", tag="v")
-            product(r[:], on_partitions, t, codes[on_free][:], scales[on_free][:], True, True)
+            multiply(r[:], part(on_partitions, slice(P * t, P * (t + 1))), part(on_free, WHOLE), True, True)
             return lambda: nc.vector.tensor_reduce(out=out_col, in_=r[:], axis=AXIS_X, op=ALU.max)
 
-        def halve(a, b, two):
+        def halve(a, b, way, two):
+            on_partitions, on_free = ((("q", a), ("k", b)), (("k", b), ("q", a)))[way]
+            low, high = HALVES
+            tiles = [slice(P * t, P * (t + 1)) for t in (2 * two, 2 * two + 1)]
             first = psum_s.tile([P, 2, HALF], F32, name="first", tag="s")
-            for i in range(2):
-                low = HALVES[0]
-                product(first[:, i, :], ("k", b), 2 * two + i, codes["q", a][:, low], scales["q", a][:, low], True, True)
+            for i, cols in enumerate(tiles):
+                multiply(first[:, i, :], part(on_partitions, cols), part(on_free, low), True, True)
             base = fold.tile([P, 2, HALF], F32, name="base")
             nc.scalar.copy(out=base[:], in_=first[:])
             step = psum_s.tile([P, 2, HALF], F32, name="step", tag="s")
-            for i in range(2):
-                high = HALVES[1]
-                product(step[:, i, :], ("k", b), 2 * two + i, codes["q", a][:, high], scales["q", a][:, high], True, False)
-                product(step[:, i, :], ("k", b), 2 * two + i, neg_codes[a][:], neg_scales[a][:], False, True)
+            for i, cols in enumerate(tiles):
+                multiply(step[:, i, :], part(on_partitions, cols), part(on_free, high), True, False)
+                if way == 1:
+                    multiply(step[:, i, :], part(on_partitions, cols), negative(a, low), False, True)
+                else:
+                    multiply(step[:, i, :], negative(a, cols), part(on_free, low), False, True)
             rise = fold.tile([P, 2, HALF], F32, name="rise")
             nc.scalar.activation(out=rise[:], in_=step[:], func=ACT.Relu)
-            tops[a, b, two] = fold.tile([P, 2, HALF], F32, name="top")
-            nc.gpsimd.tensor_tensor(out=tops[a, b, two][:], in0=base[:], in1=rise[:], op=ALU.add)
+            tops[a, b, way, two] = fold.tile([P, 2, HALF], F32, name="top")
+            nc.gpsimd.tensor_tensor(out=tops[a, b, way, two][:], in0=base[:], in1=rise[:], op=ALU.add)
             return lambda: None
 
-        def finish(a, b, two, out_cols):
-            return lambda: nc.vector.tensor_reduce(out=out_cols, in_=tops[a, b, two][:], axis=AXIS_X, op=ALU.max)
+        def finish(a, b, way, two, out_cols):
+            return lambda: nc.vector.tensor_reduce(out=out_cols, in_=tops[a, b, way, two][:], axis=AXIS_X, op=ALU.max)
 
         for h in range(2):
             turn("k", 0, h)
@@ -287,18 +300,20 @@ def tile_attention_pa_kernel(
         for c in range(TILES):
             leave_by_vector("k", 0, c)
         for h in range(2):
+            turn("k", 1, h)
+        for h in range(2):
             for j in range(TILES):
                 leave_by_scalar("q", 0, j, HALVES[h])
+        quantize_input("k", 1)
         interleave("q", 0, 0, nc.vector.tensor_copy)
         quantize("k", 0, WHOLE)
         quantize("q", 0, HALVES[0])
         interleave("q", 0, 1, nc.vector.tensor_copy)
-        for h in range(2):
-            turn("k", 1, h)
-        quantize_input("k", 1)
-        quantize("q", 0, HALVES[1])
         for j in range(TILES):
             leave_by_scalar("k", 1, j, WHOLE)
+        for h in range(2):
+            turn("q", 1, h)
+        quantize("q", 0, HALVES[1])
 
         ready = {sample: n for n, sample in enumerate(order)}
         pairs = sorted(
@@ -313,12 +328,16 @@ def tile_attention_pa_kernel(
             for sample in (("q", a), ("k", b)):
                 first_use.setdefault(sample, len(items))
             if FIRST_FOLDED <= n < len(pairs) - LAST_DIRECT:
-                for t in range(TILES):
+                first_direct = 2 if THIRD(n) else 0
+                for t in range(first_direct, TILES):
                     items.append((direct, (("q", a), ("k", b), t, row[:, t : t + 1])))
                     if t in HALVE_AT:
-                        items.append((halve, (a, b, HALVE_AT.index(t))))
-                late.append((len(items) + FINISH_LAG, finish, (a, b, 0, row[:, TILES : TILES + 2])))
-                late.append((len(items) + FINISH_LAG + FINISH_GAP, finish, (a, b, 1, row[:, TILES + 2 : 2 * TILES])))
+                        items.append((halve, (a, b, 1, HALVE_AT.index(t))))
+                if THIRD(n):
+                    items.append((halve, (a, b, 0, 0)))
+                    late.append((len(items) + FINISH_LAG, finish, (a, b, 0, 0, row[:, 0:2])))
+                late.append((len(items) + FINISH_LAG, finish, (a, b, 1, 0, row[:, TILES : TILES + 2])))
+                late.append((len(items) + FINISH_LAG + FINISH_GAP, finish, (a, b, 1, 1, row[:, TILES + 2 : 2 * TILES])))
             else:
                 for t in range(TILES):
                     items.append((direct, (("q", a), ("k", b), t, row[:, t : t + 1])))
@@ -347,13 +366,19 @@ def tile_attention_pa_kernel(
             copy = nc.vector.tensor_copy if sample in BY_VECTOR else by_gpsimd if sample in BY_GPSIMD else nc.scalar.copy
             if sample != order[2]:
                 for h in range(2):
-                    plan(use + OFFSET["turn"] + TURN_STEP * h, turn, sample + (h,))
-                plan(use + OFFSET["quantize_input"], quantize_input, sample)
+                    if sample != order[3]:
+                        plan(use + OFFSET["turn"] + TURN_STEP * h, turn, sample + (h,))
+                at = max(use + OFFSET["quantize_input"], MIN_QI)
+                plan(at, quantize_input, sample)
+                at = max(use + OFFSET["leave"], at + MIN_LEAVE)
                 for j in range(TILES):
-                    plan(use + OFFSET["leave"] + LEAVE_STEP * j // 2, leave_by_scalar, sample + (j, WHOLE))
+                    plan(at + LEAVE_STEP * j // 2, leave_by_scalar, sample + (j, WHOLE))
+                at += LEAVE_STEP * (TILES - 1) // 2
+            else:
+                at = 0
             for h in range(2):
-                plan(use + OFFSET["interleave"] + IL_STEP * h, interleave, sample + (h, copy))
-            plan(use + OFFSET["quantize"], quantize, sample + (WHOLE,))
+                plan(max(use + OFFSET["interleave"], at) + IL_STEP * h, interleave, sample + (h, copy))
+            plan(max(use + OFFSET["quantize"], at + MIN_Q), quantize, sample + (WHOLE,))
 
         consumers = []
         for n in range(len(items) + AHEAD):

@@ -77,6 +77,9 @@ def tile_attention_pa_kernel(
         psum_s = pools.enter_context(tc.psum_pool(name="psum_s", bufs=4))
         pools.enter_context(tc.manual_schedule())
 
+        zeros = const.tile([P, L], BF16)
+        nc.vector.memset(zeros[:], 0.0)
+
         states = {"k": key_states, "q": query_states}
         order = [(side, s) for s in range(SAMPLES) for side in ("k", "q")]
         x_in = {}
@@ -91,6 +94,11 @@ def tile_attention_pa_kernel(
         w_codes = {}
         w_scales = {}
         load_sample("k", 0)
+        def keep_warm(number):
+            for n in range(number):
+                unread = psum_v.tile([P, L], F32, name="unread", tag="v")
+                nc.tensor.matmul(out=unread[:], lhsT=zeros[:, 0:P], rhs=zeros[:], start=True, stop=True)
+
         bias_rows = const.tile([P, P], BF16)
         nc.vector.memset(bias_rows[:], 0.0)
         nc.sync.dma_start(out=bias_rows[0:TILES, :], in_=bk.rearrange("(j p) -> j p", p=P))
@@ -288,14 +296,17 @@ def tile_attention_pa_kernel(
         def finish(a, b, way, two, out_cols):
             return lambda: nc.vector.tensor_reduce(out=out_cols, in_=tops[a, b, way, two][:], axis=AXIS_X, op=ALU.max)
 
+        keep_warm(4)
         for h in range(2):
             turn("k", 0, h)
+        keep_warm(1)
         bias_turned = psum_s.tile([P, P], BF16, name="bias_turned", tag="s")
         nc.tensor.transpose(out=bias_turned[:], in_=bias_rows[:], identity=ident_bf16[:])
         nc.vector.tensor_copy(out=bias_cols[:], in_=bias_turned[:, 0 : 2 * TILES])
         quantize_input("k", 0)
         for h in range(2):
             turn("q", 0, h)
+        keep_warm(1)
         quantize_input("q", 0)
         for c in range(TILES):
             leave_by_vector("k", 0, c)

@@ -27,22 +27,22 @@ WHOLE = slice(0, L)
 FLOPS = 2 * 2 * SAMPLES * L * D * D + 2 * (SAMPLES * L) * (SAMPLES * L) * D
 BY_VECTOR = []
 BY_GPSIMD = []
-OFFSET = {"turn": -32, "quantize_input": -26, "leave": -18, "interleave": -10, "quantize": -3, "negate": -5, "quantize_negative": -2}
+OFFSET = {"turn": -32, "quantize_input": -26, "leave": -20, "interleave": -10, "quantize": -3, "negate": -6, "quantize_negative": -2}
 FIRST_FOLDED = 2
-LEAVE_STEP = 3
+LEAVE_STEP = 2
 THIRD = lambda n: False
-MIN_QI = 0
-MIN_LEAVE = 2
-MIN_Q = 3
+MIN_QI = 1
+MIN_LEAVE = 1
+MIN_Q = 4
 TURN_STEP = 1
 IL_STEP = 1
-NEG0 = 8
-AHEAD = 2
+NEG0 = 4
+AHEAD = 1
 AHEAD_PREP = 0
 FINISH_LAG = 8
 FINISH_GAP = 0
 LAST_DIRECT = 0
-HALVE_AT = [2, 3]
+HALVE_AT = [1, 3]
 WARM_UP = 0
 
 
@@ -72,7 +72,7 @@ def tile_attention_pa_kernel(
         inputs = pools.enter_context(tc.tile_pool(name="inputs", bufs=1))
         work = pools.enter_context(tc.tile_pool(name="work", bufs=3))
         keep = pools.enter_context(tc.tile_pool(name="keep", bufs=1))
-        fold = pools.enter_context(tc.tile_pool(name="fold", bufs=6))
+        fold = pools.enter_context(tc.tile_pool(name="fold", bufs=10))
         psum_v = pools.enter_context(tc.psum_pool(name="psum_v", bufs=4))
         psum_s = pools.enter_context(tc.psum_pool(name="psum_s", bufs=4))
         pools.enter_context(tc.manual_schedule())
@@ -391,12 +391,27 @@ def tile_attention_pa_kernel(
                 plan(max(use + OFFSET["interleave"], at) + IL_STEP * h, interleave, sample + (h, copy))
             plan(max(use + OFFSET["quantize"], at + MIN_Q), quantize, sample + (WHOLE,))
 
+        sums = []
+
+        def sum_up(which):
+            if not sums:
+                sums.append(psum_s.tile([P, SAMPLES * SAMPLES, 2 * TILES], F32, name="sums_tile", tag="s"))
+            nc.tensor.matmul(
+                out=sums[0][:, which, :].rearrange("p n c -> p (n c)"),
+                lhsT=mean_weights[:],
+                rhs=maxima[:, which, :].rearrange("p n c -> p (n c)"),
+                start=True,
+                stop=True,
+            )
+
         consumers = []
         for n in range(len(items) + AHEAD):
             for at in sorted(due):
                 if at <= n - AHEAD_PREP:
                     for stage, arguments in due.pop(at):
                         stage(*arguments)
+            if n == len(items) + AHEAD - 2:
+                sum_up(slice(0, len(pairs) - 1))
             if n >= AHEAD:
                 consumers[n - AHEAD]()
             if n < len(items):
@@ -410,19 +425,12 @@ def tile_attention_pa_kernel(
                     out=mean_weights[:], in0=mean[:], scalar1=gain[:], scalar2=0.0, op0=ALU.mult, op1=ALU.add
                 )
 
-        sums = psum_v.tile([P, SAMPLES * SAMPLES, 2 * TILES], F32, name="sums", tag="v")
-        nc.tensor.matmul(
-            out=sums[:].rearrange("p n c -> p (n c)"),
-            lhsT=mean_weights[:],
-            rhs=maxima[:].rearrange("p n c -> p (n c)"),
-            start=True,
-            stop=True,
-        )
+        sum_up(slice(len(pairs) - 1, len(pairs)))
         half = SAMPLES * SAMPLES // 2
         result = keep.tile([1, 2, 2 * half], F32)
         nc.vector.tensor_reduce(
             out=result[:, :, 0:half],
-            in_=sums[0:1, :, :].rearrange("o (r n) c -> o r n c", r=2),
+            in_=sums[0][0:1, :, :].rearrange("o (r n) c -> o r n c", r=2),
             axis=AXIS_X,
             op=ALU.add,
         )

from contextlib import ExitStack

import concourse.mybir as mybir
from concourse.masks import make_identity

F32 = mybir.dt.float32
BF16 = mybir.dt.bfloat16
I32 = mybir.dt.int32
U32 = mybir.dt.uint32
U8 = mybir.dt.uint8
FP8X4 = mybir.dt.float8_e4m3fn_x4
ACT = mybir.ActivationFunctionType
ALU = mybir.AluOpType
AXIS_X = mybir.AxisListType.X

P = 128
PACK = 4
SAMPLES = 4
L = 512
D = 512
TILES = L // P
QUADRANTS = 4

HALF = L // 2
HALVES = (slice(0, HALF), slice(HALF, L))
WHOLE = slice(0, L)
FLOPS = 2 * 2 * SAMPLES * L * D * D + 2 * (SAMPLES * L) * (SAMPLES * L) * D
BY_VECTOR = []
BY_GPSIMD = []
OFFSET = {"turn": -32, "quantize_input": -26, "leave": -20, "interleave": -10, "quantize": -3, "negate": -6, "quantize_negative": -2}
FIRST_FOLDED = 2
LEAVE_STEP = 2
THIRD = lambda n: False
MIN_QI = 1
MIN_LEAVE = 1
MIN_Q = 4
TURN_STEP = 1
IL_STEP = 1
NEG0 = 4
AHEAD = 1
AHEAD_PREP = 0
FINISH_LAG = 8
FINISH_GAP = 0
LAST_DIRECT = 0
HALVE_AT = [1, 3]
WARM_UP = 0


def load_weight_codes(nc, pool, words, name):
    codes = pool.tile([P, D], U32, name=name, align_bytes=64)
    nc.sync.dma_start(out=codes[:].bitcast(I32), in_=words[0].rearrange("p n t -> p (n t)").bitcast(I32))
    return codes


def load_weight_scales(nc, pool, scale_rows, name):
    plane = pool.tile([P, D], U8, name=name, align_bytes=64)
    nc.vector.memset(plane[:].bitcast(I32), 0)
    for quadrant in range(QUADRANTS):
        nc.sync.dma_start(
            out=plane[32 * quadrant : 32 * quadrant + 4, :].bitcast(I32),
            in_=scale_rows[0, 4 * quadrant : 4 * quadrant + 4, :].bitcast(I32),
        )
    return plane


def tile_attention_pa_kernel(
    tc, query_states, key_states, Wq_words, Wq_scales, bq, Wk_words, Wk_scales, bk, logit_scale, out
):
    nc = tc.nc
    with ExitStack() as pools:
        const = pools.enter_context(tc.tile_pool(name="const", bufs=1))
        inputs = pools.enter_context(tc.tile_pool(name="inputs", bufs=1))
        work = pools.enter_context(tc.tile_pool(name="work", bufs=3))
        keep = pools.enter_context(tc.tile_pool(name="keep", bufs=1))
        fold = pools.enter_context(tc.tile_pool(name="fold", bufs=10))
        psum_v = pools.enter_context(tc.psum_pool(name="psum_v", bufs=4))
        psum_s = pools.enter_context(tc.psum_pool(name="psum_s", bufs=4))
        pools.enter_context(tc.manual_schedule())

        zeros = const.tile([P, L], BF16)
        nc.vector.memset(zeros[:], 0.0)

        states = {"k": key_states, "q": query_states}
        order = [(side, s) for s in range(SAMPLES) for side in ("k", "q")]
        x_in = {}
        for side, s in order:
            x_in[side, s] = inputs.tile([P, TILES, D], BF16, name="x_%s%d" % (side, s))

        def load_sample(side, s):
            rows = states[side][s].rearrange("(p t) d -> p t d", t=TILES)
            for h in range(2):
                nc.sync.dma_start(out=x_in[side, s][:, 2 * h : 2 * h + 2, :], in_=rows[:, 2 * h : 2 * h + 2, :])

        w_codes = {}
        w_scales = {}
        load_sample("k", 0)
        def keep_warm(number):
            for n in range(number):
                unread = psum_v.tile([P, L], F32, name="unread", tag="v")
                nc.tensor.matmul(out=unread[:], lhsT=zeros[:, 0:P], rhs=zeros[:], start=True, stop=True)

        bias_rows = const.tile([P, P], BF16)
        nc.vector.memset(bias_rows[:], 0.0)
        nc.sync.dma_start(out=bias_rows[0:TILES, :], in_=bk.rearrange("(j p) -> j p", p=P))
        nc.sync.dma_start(out=bias_rows[TILES : 2 * TILES, :], in_=bq.rearrange("(j p) -> j p", p=P))
        load_sample("q", 0)
        w_codes["k"] = load_weight_codes(nc, const, Wk_words, "wk_codes")
        w_scales["k"] = load_weight_scales(nc, const, Wk_scales, "wk_scales")
        w_codes["q"] = load_weight_codes(nc, const, Wq_words, "wq_codes")
        w_scales["q"] = load_weight_scales(nc, const, Wq_scales, "wq_scales")
        for side, s in order[2:]:
            load_sample(side, s)
        log_gain = const.tile([P, 1], BF16)
        nc.sync.dma_start(out=log_gain[:], in_=logit_scale.partition_broadcast(P))

        ident_f32 = const.tile([P, P], F32)
        make_identity(nc, ident_f32[:])
        ident_bf16 = const.tile([P, P], BF16)
        make_identity(nc, ident_bf16[:])
        mean = const.tile([P, P], F32)
        nc.gpsimd.memset(mean[:], 1.0 / (2 * L))
        warm = const.tile([1, 1], F32)
        nc.vector.memset(warm[:], 0.0)
        nc.scalar.activation(out=warm[:], in_=warm[:], func=ACT.Exp)

        x_grouped = {}
        x_codes = {}
        x_scales = {}
        planes = {}
        grouped = {}
        codes = {}
        scales = {}
        grouped_neg = {}
        neg_codes = {}
        neg_scales = {}
        bias_cols = const.tile([P, 2 * TILES], F32)

        def bias(side):
            first = {"k": 0, "q": TILES}[side]
            return bias_cols[:, first : first + TILES]

        def turn(side, s, h):
            x_words = x_in[side, s][:].bitcast(F32)
            if h == 0:
                x_grouped[side, s] = work.tile([P, L, PACK], BF16, name="x_grouped", align_bytes=64)
            x_grouped_words = (
                x_grouped[side, s][:]
                .rearrange("p r t -> p (r t)")
                .bitcast(F32)
                .rearrange("p (h t r u) -> p h t r u", h=2, t=2, u=2)
            )
            turned = psum_s.tile([P, 2, 2, P], F32, name="turned", tag="s")
            for t in range(2):
                for u in range(2):
                    nc.tensor.transpose(
                        out=turned[:, t, u, :],
                        in_=x_words[:, 2 * h + t, u : D // 2 : 2],
                        identity=ident_f32[:],
                    )
            nc.scalar.copy(out=x_grouped_words[:, h], in_=turned[:].rearrange("p t u r -> p t r u"))

        def quantize_input(side, s):
            x_codes[side, s] = work.tile([P, L], U32, name="x_codes", align_bytes=64)
            x_scales[side, s] = work.tile([P, L], U8, name="x_scales", align_bytes=64)
            nc.vector.quantize_mx(
                out=x_codes[side, s][:].bitcast(FP8X4),
                scales=x_scales[side, s][:],
                in_=x_grouped[side, s][:].rearrange("p r t -> p (r t)"),
            )

        def project(side, s, bank, j, tokens):
            cols = slice(P * j, P * (j + 1))
            nc.tensor.matmul_mx(
                out=bank,
                lhsT=w_codes[side][:, cols].bitcast(FP8X4),
                lhsT_scale=w_scales[side][:, cols],
                rhs=x_codes[side, s][:, tokens].bitcast(FP8X4),
                rhs_scale=x_scales[side, s][:, tokens],
                start=True,
                stop=True,
            )

        def leave_by_vector(side, s, c):
            if c == 0:
                grouped[side, s] = work.tile([P, L, PACK], BF16, name="grouped", align_bytes=64)
            tokens = slice(P * c, P * (c + 1))
            projected = psum_v.tile([P, TILES, P], F32, name="projected", tag="v")
            for j in range(TILES):
                project(side, s, projected[:, j, :], j, tokens)
            nc.vector.tensor_tensor(
                out=grouped[side, s][:, tokens, :],
                in0=projected[:].rearrange("p j r -> p r j"),
                in1=bias(side).unsqueeze(1).to_broadcast([P, P, PACK]),
                op=ALU.add,
            )

        def leave_by_scalar(side, s, j, tokens):
            if (side, s) not in planes:
                planes[side, s] = work.tile([P, TILES, L], BF16, name="planes")
            projected = psum_s.tile([P, tokens.stop - tokens.start], F32, name="projected", tag="s")
            project(side, s, projected[:], j, tokens)
            nc.scalar.activation(
                out=planes[side, s][:, j, tokens],
                in_=projected[:],
                func=ACT.Identity,
                bias=bias(side)[:, j : j + 1],
                scale=1.0,
            )

        def interleave(side, s, h, copy):
            if h == 0:
                grouped[side, s] = work.tile([P, L, PACK], BF16, name="grouped", align_bytes=64)
            tokens = HALVES[h]
            copy(
                out=grouped[side, s][:, tokens, :].rearrange("p (c i) t -> p c t i", i=4),
                in_=planes[side, s][:, :, tokens].rearrange("p t (c i) -> p c t i", i=4),
            )

        def quantize(side, s, tokens):
            if (side, s) not in codes:
                codes[side, s] = keep.tile([P, L], U32, name="codes_%s%d" % (side, s), align_bytes=64)
                scales[side, s] = keep.tile([P, L], U8, name="scales_%s%d" % (side, s), align_bytes=64)
            nc.vector.quantize_mx(
                out=codes[side, s][:, tokens].bitcast(FP8X4),
                scales=scales[side, s][:, tokens],
                in_=grouped[side, s][:, tokens, :].rearrange("p r t -> p (r t)"),
            )

        def negate(s):
            grouped_neg[s] = work.tile([P, HALF, PACK], BF16, name="grouped_neg", align_bytes=64)
            nc.gpsimd.tensor_scalar(
                out=grouped_neg[s][:],
                in0=grouped["q", s][:, HALVES[0], :],
                scalar1=-1.0,
                scalar2=0.0,
                op0=ALU.mult,
                op1=ALU.add,
            )

        def quantize_negative(s):
            neg_codes[s] = keep.tile([P, HALF], U32, name="neg_codes_%d" % s, align_bytes=64)
            neg_scales[s] = keep.tile([P, HALF], U8, name="neg_scales_%d" % s, align_bytes=64)
            nc.vector.quantize_mx(
                out=neg_codes[s][:].bitcast(FP8X4),
                scales=neg_scales[s][:],
                in_=grouped_neg[s][:].rearrange("p r t -> p (r t)"),
            )

        maxima = keep.tile([P, SAMPLES * SAMPLES, 2 * TILES], F32)
        tops = {}

        def part(sample, cols):
            return codes[sample][:, cols], scales[sample][:, cols]

        def negative(s, cols):
            return neg_codes[s][:, cols], neg_scales[s][:, cols]

        def multiply(bank, stationary, moving, start, stop):
            nc.tensor.matmul_mx(
                out=bank,
                lhsT=stationary[0].bitcast(FP8X4),
                lhsT_scale=stationary[1],
                rhs=moving[0].bitcast(FP8X4),
                rhs_scale=moving[1],
                start=start,
                stop=stop,
            )

        def direct(on_partitions, on_free, t, out_col):
            r = psum_v.tile([P, L], F32, name="r", tag="v")
            multiply(r[:], part(on_partitions, slice(P * t, P * (t + 1))), part(on_free, WHOLE), True, True)
            return lambda: nc.vector.tensor_reduce(out=out_col, in_=r[:], axis=AXIS_X, op=ALU.max)

        def halve(a, b, way, two):
            on_partitions, on_free = ((("q", a), ("k", b)), (("k", b), ("q", a)))[way]
            low, high = HALVES
            tiles = [slice(P * t, P * (t + 1)) for t in (2 * two, 2 * two + 1)]
            first = psum_s.tile([P, 2, HALF], F32, name="first", tag="s")
            for i, cols in enumerate(tiles):
                multiply(first[:, i, :], part(on_partitions, cols), part(on_free, low), True, True)
            base = fold.tile([P, 2, HALF], F32, name="base")
            nc.scalar.copy(out=base[:], in_=first[:])
            step = psum_s.tile([P, 2, HALF], F32, name="step", tag="s")
            for i, cols in enumerate(tiles):
                multiply(step[:, i, :], part(on_partitions, cols), part(on_free, high), True, False)
                if way == 1:
                    multiply(step[:, i, :], part(on_partitions, cols), negative(a, low), False, True)
                else:
                    multiply(step[:, i, :], negative(a, cols), part(on_free, low), False, True)
            rise = fold.tile([P, 2, HALF], F32, name="rise")
            nc.scalar.activation(out=rise[:], in_=step[:], func=ACT.Relu)
            tops[a, b, way, two] = fold.tile([P, 2, HALF], F32, name="top")
            nc.gpsimd.tensor_tensor(out=tops[a, b, way, two][:], in0=base[:], in1=rise[:], op=ALU.add)
            return lambda: None

        def finish(a, b, way, two, out_cols):
            return lambda: nc.vector.tensor_reduce(out=out_cols, in_=tops[a, b, way, two][:], axis=AXIS_X, op=ALU.max)

        keep_warm(4)
        for h in range(2):
            turn("k", 0, h)
        keep_warm(1)
        bias_turned = psum_s.tile([P, P], BF16, name="bias_turned", tag="s")
        nc.tensor.transpose(out=bias_turned[:], in_=bias_rows[:], identity=ident_bf16[:])
        nc.vector.tensor_copy(out=bias_cols[:], in_=bias_turned[:, 0 : 2 * TILES])
        quantize_input("k", 0)
        for h in range(2):
            turn("q", 0, h)
        keep_warm(1)
        quantize_input("q", 0)
        for c in range(TILES):
            leave_by_vector("k", 0, c)
        for h in range(2):
            turn("k", 1, h)
        for h in range(2):
            for j in range(TILES):
                leave_by_scalar("q", 0, j, HALVES[h])
        quantize_input("k", 1)
        interleave("q", 0, 0, nc.vector.tensor_copy)
        quantize("k", 0, WHOLE)
        quantize("q", 0, HALVES[0])
        interleave("q", 0, 1, nc.vector.tensor_copy)
        for j in range(TILES):
            leave_by_scalar("k", 1, j, WHOLE)
        for h in range(2):
            turn("q", 1, h)
        quantize("q", 0, HALVES[1])

        ready = {sample: n for n, sample in enumerate(order)}
        pairs = sorted(
            [(a, b) for a in range(SAMPLES) for b in range(SAMPLES)],
            key=lambda ab: (max(ready["q", ab[0]], ready["k", ab[1]]), ab),
        )
        items = []
        late = []
        first_use = {}
        for n, (a, b) in enumerate(pairs):
            row = maxima[:, SAMPLES * a + b, :]
            for sample in (("q", a), ("k", b)):
                first_use.setdefault(sample, len(items))
            if FIRST_FOLDED <= n < len(pairs) - LAST_DIRECT:
                first_direct = 2 if THIRD(n) else 0
                for t in range(first_direct, TILES):
                    items.append((direct, (("q", a), ("k", b), t, row[:, t : t + 1])))
                    if t in HALVE_AT:
                        items.append((halve, (a, b, 1, HALVE_AT.index(t))))
                if THIRD(n):
                    items.append((halve, (a, b, 0, 0)))
                    late.append((len(items) + FINISH_LAG, finish, (a, b, 0, 0, row[:, 0:2])))
                late.append((len(items) + FINISH_LAG, finish, (a, b, 1, 0, row[:, TILES : TILES + 2])))
                late.append((len(items) + FINISH_LAG + FINISH_GAP, finish, (a, b, 1, 1, row[:, TILES + 2 : 2 * TILES])))
            else:
                for t in range(TILES):
                    items.append((direct, (("q", a), ("k", b), t, row[:, t : t + 1])))
                for t in range(TILES):
                    col = TILES + t
                    items.append((direct, (("k", b), ("q", a), t, row[:, col : col + 1])))
            while late and late[0][0] <= len(items):
                items.append(late.pop(0)[1:])
        items += [entry[1:] for entry in late]

        def by_gpsimd(out, in_):
            nc.gpsimd.tensor_scalar(out=out, in0=in_, scalar1=1.0, scalar2=0.0, op0=ALU.mult, op1=ALU.add)

        due = {}

        def plan(n, stage, arguments):
            due.setdefault(n, []).append((stage, arguments))

        for sample in order[1:]:
            use = first_use[sample]
            if sample[0] == "q":
                plan(use + OFFSET["negate"] if sample[1] > 0 else NEG0, negate, sample[1:])
                plan(use + OFFSET["quantize_negative"] if sample[1] > 0 else NEG0 + 4, quantize_negative, sample[1:])
        for sample in order[2:]:
            use = first_use[sample]
            copy = nc.vector.tensor_copy if sample in BY_VECTOR else by_gpsimd if sample in BY_GPSIMD else nc.scalar.copy
            if sample != order[2]:
                for h in range(2):
                    if sample != order[3]:
                        plan(use + OFFSET["turn"] + TURN_STEP * h, turn, sample + (h,))
                at = max(use + OFFSET["quantize_input"], MIN_QI)
                plan(at, quantize_input, sample)
                at = max(use + OFFSET["leave"], at + MIN_LEAVE)
                for j in range(TILES):
                    plan(at + LEAVE_STEP * j // 2, leave_by_scalar, sample + (j, WHOLE))
                at += LEAVE_STEP * (TILES - 1) // 2
            else:
                at = 0
            for h in range(2):
                plan(max(use + OFFSET["interleave"], at) + IL_STEP * h, interleave, sample + (h, copy))
            plan(max(use + OFFSET["quantize"], at + MIN_Q), quantize, sample + (WHOLE,))

        sums = []

        def sum_up(which):
            if not sums:
                sums.append(psum_s.tile([P, SAMPLES * SAMPLES, 2 * TILES], F32, name="sums_tile", tag="s"))
            nc.tensor.matmul(
                out=sums[0][:, which, :].rearrange("p n c -> p (n c)"),
                lhsT=mean_weights[:],
                rhs=maxima[:, which, :].rearrange("p n c -> p (n c)"),
                start=True,
                stop=True,
            )

        consumers = []
        for n in range(len(items) + AHEAD):
            for at in sorted(due):
                if at <= n - AHEAD_PREP:
                    for stage, arguments in due.pop(at):
                        stage(*arguments)
            if n == len(items) + AHEAD - 2:
                sum_up(slice(0, len(pairs) - 1))
            if n >= AHEAD:
                consumers[n - AHEAD]()
            if n < len(items):
                stage, arguments = items[n]
                consumers.append(stage(*arguments))
            if n == 0:
                gain = const.tile([P, 1], F32)
                nc.scalar.activation(out=gain[:], in_=log_gain[:], func=ACT.Exp)
                mean_weights = const.tile([P, P], F32)
                nc.gpsimd.tensor_scalar(
                    out=mean_weights[:], in0=mean[:], scalar1=gain[:], scalar2=0.0, op0=ALU.mult, op1=ALU.add
                )

        sum_up(slice(len(pairs) - 1, len(pairs)))
        half = SAMPLES * SAMPLES // 2
        result = keep.tile([1, 2, 2 * half], F32)
        nc.vector.tensor_reduce(
            out=result[:, :, 0:half],
            in_=sums[0][0:1, :, :].rearrange("o (r n) c -> o r n c", r=2),
            axis=AXIS_X,
            op=ALU.add,
        )
        nc.sync.dma_start(out=out.rearrange("(o r a) b -> o r (a b)", o=1, r=2), in_=result[:, :, 0:half])
